import numpy as np
import ml_dtypes


def mxq(x, axis, fmt="e4m3"):
    dtype, down = {"e4m3": (ml_dtypes.float8_e4m3fn, 7), "e5m2": (ml_dtypes.float8_e5m2, 14)}[fmt]
    v = np.moveaxis(np.asarray(x, np.float32).astype(ml_dtypes.bfloat16).astype(np.float64), axis, -1)
    blocks = v.reshape(v.shape[:-1] + (-1, 32))
    amax = np.abs(blocks).max(-1, keepdims=True)
    byte = np.maximum(np.where(amax > 0, np.frexp(amax)[1] - 1 + 127, 0) - down, 1)
    scale = np.exp2(byte - 127.0)
    codes = (blocks / scale).astype(np.float32).astype(dtype).astype(np.float64)
    return np.moveaxis((codes * scale).reshape(v.shape), -1, axis)


WIDE = False


def mx_kscale(k):
    if not WIDE:
        return np.ones(k)
    levels = np.array([10, -10, 5, -5, 0])
    a = np.random.permutation(np.resize(levels, k // 512 * 4)).reshape(k // 512, 4)
    idx = np.arange(k)
    return np.exp2(a[idx // 512, idx % 128 // 32])


BF16 = ml_dtypes.bfloat16


def bf(x):
    return np.asarray(x, np.float32).astype(BF16)


def f64(x):
    return np.asarray(x).astype(np.float64)


B, N, NFEAT, NHID, NHID2, NCLASS = 2, 1024, 512, 512, 1024, 256


def setup_inputs():
    t, s = mx_kscale(NFEAT), mx_kscale(N)
    return {"x": bf(np.random.standard_normal((B, N, NFEAT)) * t / s[:, None]),
            "adj": bf(np.random.uniform(size=(N, N)) * s),
            "S": bf(np.random.standard_normal((N, N)) * 1.7 / np.sqrt(N)),
            "W1": bf(np.random.standard_normal((NFEAT, NHID)) / np.sqrt(NFEAT) / t[:, None])}


def reference(x, adj, S, W1):
    support = mxq(f64(x), 2, "e4m3") @ mxq(f64(W1), 0, "e4m3")
    weighting = f64(adj) * f64(S)
    out = mxq(weighting, 1, "e4m3") @ mxq(support, 1, "e4m3")
    return np.maximum(out, 0.0)

@@ -1,0 +1,169 @@
+from contextlib import ExitStack
+
+import concourse.mybir as mybir
+from concourse.masks import make_identity
+
+BF16 = mybir.dt.bfloat16
+F32 = mybir.dt.float32
+U32 = mybir.dt.uint32
+U8 = mybir.dt.uint8
+FP8X4 = mybir.dt.float8_e4m3fn_x4
+
+P = 128
+PACK = 4
+K_PASS = P * PACK
+
+BATCH = 2
+NODES = 1024
+FEATURES = 512
+HIDDEN = 512
+NODE_PASSES = NODES // K_PASS
+HALVES = BATCH * NODE_PASSES
+NODE_TILES = NODES // P
+HIDDEN_QUARTERS = HIDDEN // P
+
+FLOPS = 2 * BATCH * NODES * FEATURES * HIDDEN + 2 * BATCH * NODES * NODES * HIDDEN
+
+
+def tile_gcn_pa_kernel(tc, x, adj, S, W1, out):
+    nc = tc.nc
+    relu = mybir.ActivationFunctionType.Relu
+
+    with ExitStack() as ctx:
+        keep = ctx.enter_context(tc.tile_pool(name="keep", bufs=1))
+        tr_psum = ctx.enter_context(tc.psum_pool(name="tr_psum", bufs=4))
+        mm_psum = ctx.enter_context(tc.psum_pool(name="mm_psum", bufs=4))
+
+        w1_rows = keep.tile([P, PACK, HIDDEN], BF16, name="w1_rows")
+        nc.sync.dma_start(
+            out=w1_rows[:].rearrange("q (u e) h -> q u e h", u=2),
+            in_=W1.rearrange("(u q e) h -> q u e h", u=2, e=2),
+        )
+        x_view = x.rearrange("b (g u p e) k -> b g p u e k", g=NODE_PASSES, u=2, e=2)
+        x_rows = []
+        for i in range(HALVES):
+            rows = keep.tile([P, PACK, FEATURES], BF16, name="x_rows%d" % i)
+            nc.sync.dma_start(
+                out=rows[:].rearrange("p (u e) k -> p u e k", u=2),
+                in_=x_view[i // NODE_PASSES, i % NODE_PASSES],
+            )
+            x_rows.append(rows)
+        adj_rows = []
+        s_rows = []
+        for n in range(NODE_TILES):
+            a = keep.tile([P, NODES], BF16, name="adj_rows%d" % n)
+            nc.sync.dma_start(out=a[:], in_=adj[n * P : (n + 1) * P, :])
+            adj_rows.append(a)
+            s = keep.tile([P, NODES], BF16, name="s_rows%d" % n)
+            nc.sync.dma_start(out=s[:], in_=S[n * P : (n + 1) * P, :])
+            s_rows.append(s)
+
+        ident = keep.tile([P, P], F32, name="ident")
+        make_identity(nc, ident[:])
+
+        w1_grouped = keep.tile([P, HIDDEN, PACK], BF16, name="w1_grouped", align_bytes=64)
+        nc.vector.tensor_copy(
+            out=w1_grouped[:].rearrange("q (c i) t -> q c t i", i=4),
+            in_=w1_rows[:].rearrange("q t (c i) -> q c t i", i=4),
+        )
+        w1_codes = keep.tile([P, HIDDEN], U32, name="w1_codes", align_bytes=64)
+        w1_scales = keep.tile([P, HIDDEN], U8, name="w1_scales", align_bytes=64)
+        nc.vector.quantize_mx(
+            out=w1_codes[:].bitcast(FP8X4),
+            scales=w1_scales[:],
+            in_=w1_grouped[:].rearrange("q h t -> q (h t)"),
+        )
+
+        def empty_bank(index, dst, src):
+            if index % 4 == 3:
+                nc.vector.tensor_copy(out=dst, in_=src)
+            else:
+                nc.scalar.copy(out=dst, in_=src)
+
+        sup_codes = []
+        sup_scales = []
+        for i in range(HALVES):
+            x_grouped = keep.tile([P, PACK, P, PACK], BF16, name="x_grouped%d" % i, align_bytes=64)
+            for u in range(2):
+                xt = tr_psum.tile([P, 2, 2, P], F32, tag="tr", name="xt")
+                for e in range(2):
+                    words = x_rows[i][:, 2 * u + e, :].bitcast(F32)
+                    for uk in range(2):
+                        nc.tensor.transpose(xt[:, e, uk, :], words[:, uk * P : (uk + 1) * P], ident[:])
+                empty_bank(
+                    2 * i + u,
+                    x_grouped[:, 2 * u : 2 * u + 2, :, :].bitcast(F32),
+                    xt[:].rearrange("q e uk m -> q e m uk"),
+                )
+            x_codes = keep.tile([P, K_PASS], U32, name="x_codes%d" % i, align_bytes=64)
+            x_scales = keep.tile([P, K_PASS], U8, name="x_scales%d" % i, align_bytes=64)
+            nc.vector.quantize_mx(
+                out=x_codes[:].bitcast(FP8X4),
+                scales=x_scales[:],
+                in_=x_grouped[:].rearrange("q j m t -> q (j m t)"),
+            )
+            sup_grouped = keep.tile([P, HIDDEN, PACK], BF16, name="sup_grouped%d" % i, align_bytes=64)
+            for hq in range(HIDDEN_QUARTERS):
+                h_cols = slice(hq * P, (hq + 1) * P)
+                sup_ps = mm_psum.tile([P, PACK, P], F32, tag="mm", name="sup_ps")
+                for j in range(PACK):
+                    m_cols = slice(j * P, (j + 1) * P)
+                    nc.tensor.matmul_mx(
+                        out=sup_ps[:, j, :],
+                        lhsT=x_codes[:, m_cols].bitcast(FP8X4),
+                        lhsT_scale=x_scales[:, m_cols],
+                        rhs=w1_codes[:, h_cols].bitcast(FP8X4),
+                        rhs_scale=w1_scales[:, h_cols],
+                        start=True,
+                        stop=True,
+                    )
+                empty_bank(hq, sup_grouped[:, h_cols, :], sup_ps[:].rearrange("p j h -> p h j"))
+            codes = keep.tile([P, HIDDEN], U32, name="sup_codes%d" % i, align_bytes=64)
+            scales = keep.tile([P, HIDDEN], U8, name="sup_scales%d" % i, align_bytes=64)
+            nc.vector.quantize_mx(
+                out=codes[:].bitcast(FP8X4),
+                scales=scales[:],
+                in_=sup_grouped[:].rearrange("p h j -> p (h j)"),
+            )
+            sup_codes.append(codes)
+            sup_scales.append(scales)
+
+        for n in range(NODE_TILES):
+            w_rows = keep.tile([P, NODES], BF16, name="w_rows%d" % n)
+            nc.vector.tensor_tensor(
+                out=w_rows[:], in0=adj_rows[n][:], in1=s_rows[n][:], op=mybir.AluOpType.mult
+            )
+            wt = tr_psum.tile([P, NODE_PASSES, 2, P], F32, tag="tr", name="wt")
+            words = w_rows[:].bitcast(F32)
+            for g in range(NODE_PASSES):
+                for u in range(2):
+                    c = (2 * g + u) * P
+                    nc.tensor.transpose(wt[:, g, u, :], words[:, c : c + P], ident[:])
+            w_grouped = keep.tile([P, NODE_PASSES, P, PACK], BF16, name="w_grouped%d" % n, align_bytes=64)
+            empty_bank(n, w_grouped[:].bitcast(F32), wt[:].rearrange("p g u n -> p g n u"))
+            w_codes = keep.tile([P, NODE_PASSES * P], U32, name="w_codes%d" % n, align_bytes=64)
+            w_scales = keep.tile([P, NODE_PASSES * P], U8, name="w_scales%d" % n, align_bytes=64)
+            nc.vector.quantize_mx(
+                out=w_codes[:].bitcast(FP8X4),
+                scales=w_scales[:],
+                in_=w_grouped[:].rearrange("p g n t -> p (g n t)"),
+            )
+            for b in range(BATCH):
+                out_ps = mm_psum.tile([P, HIDDEN], F32, tag="mm", name="out_ps")
+                for g in range(NODE_PASSES):
+                    n_cols = slice(g * P, (g + 1) * P)
+                    nc.tensor.matmul_mx(
+                        out=out_ps[:],
+                        lhsT=w_codes[:, n_cols].bitcast(FP8X4),
+                        lhsT_scale=w_scales[:, n_cols],
+                        rhs=sup_codes[NODE_PASSES * b + g][:].bitcast(FP8X4),
+                        rhs_scale=sup_scales[NODE_PASSES * b + g][:],
+                        start=(g == 0),
+                        stop=(g == NODE_PASSES - 1),
+                    )
+                result = keep.tile([P, HIDDEN], F32, name="result%d_%d" % (n, b))
+                if (2 * n + b) % 4 == 3:
+                    nc.vector.tensor_scalar_max(out=result[:], in0=out_ps[:], scalar1=0.0)
+                else:
+                    nc.scalar.activation(out=result[:], in_=out_ps[:], func=relu)
+                nc.sync.dma_start(out=out[b, n * P : (n + 1) * P, :], in_=result[:])

@@ -20,16 +20,17 @@ HIDDEN = 512
 NODE_PASSES = NODES // K_PASS
 HALVES = BATCH * NODE_PASSES
 NODE_TILES = NODES // P
-HIDDEN_QUARTERS = HIDDEN // P
+PAIRS = NODE_TILES // 2
+QUARTERS = HIDDEN // P
 
 FLOPS = 2 * BATCH * NODES * FEATURES * HIDDEN + 2 * BATCH * NODES * NODES * HIDDEN
 
 
 def tile_gcn_pa_kernel(tc, x, adj, S, W1, out):
     nc = tc.nc
-    relu = mybir.ActivationFunctionType.Relu
 
     with ExitStack() as ctx:
+        ctx.enter_context(tc.manual_schedule())
         keep = ctx.enter_context(tc.tile_pool(name="keep", bufs=1))
         tr_psum = ctx.enter_context(tc.psum_pool(name="tr_psum", bufs=4))
         mm_psum = ctx.enter_context(tc.psum_pool(name="mm_psum", bufs=4))
@@ -48,14 +49,17 @@ def tile_gcn_pa_kernel(tc, x, adj, S, W1, out):
                 in_=x_view[i // NODE_PASSES, i % NODE_PASSES],
             )
             x_rows.append(rows)
+        adj_view = adj.rearrange("(p t) m -> p t m", t=NODE_TILES)
+        s_view = S.rearrange("(p t) m -> p t m", t=NODE_TILES)
+        out_view = out.rearrange("b (p t) h -> b p t h", t=NODE_TILES)
         adj_rows = []
         s_rows = []
-        for n in range(NODE_TILES):
-            a = keep.tile([P, NODES], BF16, name="adj_rows%d" % n)
-            nc.sync.dma_start(out=a[:], in_=adj[n * P : (n + 1) * P, :])
+        for r in range(PAIRS):
+            a = keep.tile([P, 2, NODES], BF16, name="adj_rows%d" % r)
+            nc.sync.dma_start(out=a[:], in_=adj_view[:, 2 * r : 2 * r + 2, :])
             adj_rows.append(a)
-            s = keep.tile([P, NODES], BF16, name="s_rows%d" % n)
-            nc.sync.dma_start(out=s[:], in_=S[n * P : (n + 1) * P, :])
+            s = keep.tile([P, 2, NODES], BF16, name="s_rows%d" % r)
+            nc.sync.dma_start(out=s[:], in_=s_view[:, 2 * r : 2 * r + 2, :])
             s_rows.append(s)
 
         ident = keep.tile([P, P], F32, name="ident")
@@ -74,96 +78,160 @@ def tile_gcn_pa_kernel(tc, x, adj, S, W1, out):
             in_=w1_grouped[:].rearrange("q h t -> q (h t)"),
         )
 
-        def empty_bank(index, dst, src):
-            if index % 4 == 3:
-                nc.vector.tensor_copy(out=dst, in_=src)
-            else:
-                nc.scalar.copy(out=dst, in_=src)
+        def quantise(name, grouped):
+            codes = keep.tile([P, K_PASS], U32, name=name + "_codes", align_bytes=64)
+            scales = keep.tile([P, K_PASS], U8, name=name + "_scales", align_bytes=64)
+            nc.vector.quantize_mx(out=codes[:].bitcast(FP8X4), scales=scales[:], in_=grouped)
+            return codes, scales
 
-        sup_codes = []
-        sup_scales = []
-        for i in range(HALVES):
-            x_grouped = keep.tile([P, PACK, P, PACK], BF16, name="x_grouped%d" % i, align_bytes=64)
+        def transpose_words(rows):
+            bank = tr_psum.tile([P, PACK, P], F32, tag="tr", name="tr_bank")
+            for c in range(PACK):
+                nc.tensor.transpose(bank[:, c, :], rows[:, c * P : (c + 1) * P], ident[:])
+            return bank
+
+        x_banks = {}
+        x_grouped = {}
+        x_q = {}
+        sup_banks = {}
+        sup_grouped = {}
+        sup_q = {}
+
+        def transpose_x(i):
+            words = x_rows[i][:].bitcast(F32)
+            x_banks[i] = [
+                transpose_words(words[:, 2 * u : 2 * u + 2, :].rearrange("p e w -> p (e w)")) for u in range(2)
+            ]
+
+        def copy_x(i):
+            x_grouped[i] = keep.tile([P, PACK, P, PACK], BF16, name="x_grouped%d" % i, align_bytes=64)
             for u in range(2):
-                xt = tr_psum.tile([P, 2, 2, P], F32, tag="tr", name="xt")
-                for e in range(2):
-                    words = x_rows[i][:, 2 * u + e, :].bitcast(F32)
-                    for uk in range(2):
-                        nc.tensor.transpose(xt[:, e, uk, :], words[:, uk * P : (uk + 1) * P], ident[:])
-                empty_bank(
-                    2 * i + u,
-                    x_grouped[:, 2 * u : 2 * u + 2, :, :].bitcast(F32),
-                    xt[:].rearrange("q e uk m -> q e m uk"),
+                nc.scalar.copy(
+                    out=x_grouped[i][:, 2 * u : 2 * u + 2, :, :].bitcast(F32),
+                    in_=x_banks[i][u][:].rearrange("q (e uk) m -> q e m uk", e=2),
                 )
-            x_codes = keep.tile([P, K_PASS], U32, name="x_codes%d" % i, align_bytes=64)
-            x_scales = keep.tile([P, K_PASS], U8, name="x_scales%d" % i, align_bytes=64)
-            nc.vector.quantize_mx(
-                out=x_codes[:].bitcast(FP8X4),
-                scales=x_scales[:],
-                in_=x_grouped[:].rearrange("q j m t -> q (j m t)"),
-            )
-            sup_grouped = keep.tile([P, HIDDEN, PACK], BF16, name="sup_grouped%d" % i, align_bytes=64)
-            for hq in range(HIDDEN_QUARTERS):
+
+        def quantise_x(i):
+            x_q[i] = quantise("x%d" % i, x_grouped[i][:].rearrange("q j m t -> q (j m t)"))
+
+        def support_matmuls(i):
+            codes, scales = x_q[i]
+            sup_banks[i] = []
+            for hq in range(QUARTERS):
                 h_cols = slice(hq * P, (hq + 1) * P)
-                sup_ps = mm_psum.tile([P, PACK, P], F32, tag="mm", name="sup_ps")
+                bank = mm_psum.tile([P, PACK, P], F32, tag="mm", name="sup_bank")
                 for j in range(PACK):
                     m_cols = slice(j * P, (j + 1) * P)
                     nc.tensor.matmul_mx(
-                        out=sup_ps[:, j, :],
-                        lhsT=x_codes[:, m_cols].bitcast(FP8X4),
-                        lhsT_scale=x_scales[:, m_cols],
+                        out=bank[:, j, :],
+                        lhsT=codes[:, m_cols].bitcast(FP8X4),
+                        lhsT_scale=scales[:, m_cols],
                         rhs=w1_codes[:, h_cols].bitcast(FP8X4),
                         rhs_scale=w1_scales[:, h_cols],
                         start=True,
                         stop=True,
                     )
-                empty_bank(hq, sup_grouped[:, h_cols, :], sup_ps[:].rearrange("p j h -> p h j"))
-            codes = keep.tile([P, HIDDEN], U32, name="sup_codes%d" % i, align_bytes=64)
-            scales = keep.tile([P, HIDDEN], U8, name="sup_scales%d" % i, align_bytes=64)
-            nc.vector.quantize_mx(
-                out=codes[:].bitcast(FP8X4),
-                scales=scales[:],
-                in_=sup_grouped[:].rearrange("p h j -> p (h j)"),
-            )
-            sup_codes.append(codes)
-            sup_scales.append(scales)
+                sup_banks[i].append(bank)
 
-        for n in range(NODE_TILES):
-            w_rows = keep.tile([P, NODES], BF16, name="w_rows%d" % n)
-            nc.vector.tensor_tensor(
-                out=w_rows[:], in0=adj_rows[n][:], in1=s_rows[n][:], op=mybir.AluOpType.mult
-            )
-            wt = tr_psum.tile([P, NODE_PASSES, 2, P], F32, tag="tr", name="wt")
-            words = w_rows[:].bitcast(F32)
-            for g in range(NODE_PASSES):
-                for u in range(2):
-                    c = (2 * g + u) * P
-                    nc.tensor.transpose(wt[:, g, u, :], words[:, c : c + P], ident[:])
-            w_grouped = keep.tile([P, NODE_PASSES, P, PACK], BF16, name="w_grouped%d" % n, align_bytes=64)
-            empty_bank(n, w_grouped[:].bitcast(F32), wt[:].rearrange("p g u n -> p g n u"))
-            w_codes = keep.tile([P, NODE_PASSES * P], U32, name="w_codes%d" % n, align_bytes=64)
-            w_scales = keep.tile([P, NODE_PASSES * P], U8, name="w_scales%d" % n, align_bytes=64)
-            nc.vector.quantize_mx(
-                out=w_codes[:].bitcast(FP8X4),
-                scales=w_scales[:],
-                in_=w_grouped[:].rearrange("p g n t -> p (g n t)"),
-            )
-            for b in range(BATCH):
-                out_ps = mm_psum.tile([P, HIDDEN], F32, tag="mm", name="out_ps")
-                for g in range(NODE_PASSES):
-                    n_cols = slice(g * P, (g + 1) * P)
-                    nc.tensor.matmul_mx(
-                        out=out_ps[:],
-                        lhsT=w_codes[:, n_cols].bitcast(FP8X4),
-                        lhsT_scale=w_scales[:, n_cols],
-                        rhs=sup_codes[NODE_PASSES * b + g][:].bitcast(FP8X4),
-                        rhs_scale=sup_scales[NODE_PASSES * b + g][:],
-                        start=(g == 0),
-                        stop=(g == NODE_PASSES - 1),
-                    )
-                result = keep.tile([P, HIDDEN], F32, name="result%d_%d" % (n, b))
-                if (2 * n + b) % 4 == 3:
-                    nc.vector.tensor_scalar_max(out=result[:], in0=out_ps[:], scalar1=0.0)
+        def copy_support(i):
+            sup_grouped[i] = keep.tile([P, HIDDEN, PACK], BF16, name="sup_grouped%d" % i, align_bytes=64)
+            first_on_vector = 2 if i < NODE_PASSES else 3
+            for hq in range(QUARTERS):
+                dst = sup_grouped[i][:, hq * P : (hq + 1) * P, :]
+                src = sup_banks[i][hq][:].rearrange("p j h -> p h j")
+                if hq >= first_on_vector:
+                    nc.vector.tensor_copy(out=dst, in_=src)
                 else:
-                    nc.scalar.activation(out=result[:], in_=out_ps[:], func=relu)
-                nc.sync.dma_start(out=out[b, n * P : (n + 1) * P, :], in_=result[:])
+                    nc.scalar.copy(out=dst, in_=src)
+
+        def quantise_support(i):
+            sup_q[i] = quantise("sup%d" % i, sup_grouped[i][:].rearrange("p h j -> p (h j)"))
+
+        w_rows = {}
+        w_banks = {}
+        w_grouped = {}
+        w_q = {}
+        out_banks = {}
+
+        def product(r):
+            w_rows[r] = keep.tile([P, 2, NODES], BF16, name="w_rows%d" % r)
+            nc.vector.tensor_tensor(
+                out=w_rows[r][:], in0=adj_rows[r][:], in1=s_rows[r][:], op=mybir.AluOpType.mult
+            )
+
+        def transpose_w(r):
+            words = w_rows[r][:].bitcast(F32)
+            w_banks[r] = [transpose_words(words[:, t, :]) for t in range(2)]
+
+        def copy_w(r):
+            w_grouped[r] = keep.tile([P, 2, NODE_PASSES, P, PACK], BF16, name="w_grouped%d" % r, align_bytes=64)
+            for t in range(2):
+                nc.scalar.copy(
+                    out=w_grouped[r][:, t, :, :, :].bitcast(F32),
+                    in_=w_banks[r][t][:].rearrange("p (g u) n -> p g n u", g=NODE_PASSES),
+                )
+
+        def quantise_w(r):
+            w_q[r] = quantise("w%d" % r, w_grouped[r][:].rearrange("p t g n v -> p (t g n v)"))
+
+        def output_matmuls(r):
+            codes, scales = w_q[r]
+            for b in range(BATCH):
+                for t in range(2):
+                    bank = mm_psum.tile([P, HIDDEN], F32, tag="mm", name="out_bank")
+                    for g in range(NODE_PASSES):
+                        n_cols = slice((t * NODE_PASSES + g) * P, (t * NODE_PASSES + g + 1) * P)
+                        s_codes, s_scales = sup_q[b * NODE_PASSES + g]
+                        nc.tensor.matmul_mx(
+                            out=bank[:],
+                            lhsT=codes[:, n_cols].bitcast(FP8X4),
+                            lhsT_scale=scales[:, n_cols],
+                            rhs=s_codes[:].bitcast(FP8X4),
+                            rhs_scale=s_scales[:],
+                            start=(g == 0),
+                            stop=(g == NODE_PASSES - 1),
+                        )
+                    out_banks[(r, b, t)] = bank
+
+        def relu_and_store(r):
+            for b in range(BATCH):
+                result = keep.tile([P, 2, HIDDEN], F32, name="result%d_%d" % (r, b))
+                nc.scalar.activation(
+                    out=result[:, 0, :], in_=out_banks[(r, b, 0)][:], func=mybir.ActivationFunctionType.Relu
+                )
+                nc.vector.tensor_scalar_max(out=result[:, 1, :], in0=out_banks[(r, b, 1)][:], scalar1=0.0)
+                nc.sync.dma_start(out=out_view[b, :, 2 * r : 2 * r + 2, :], in_=result[:])
+
+        transpose_x(0)
+        copy_x(0)
+        transpose_x(1)
+        copy_x(1)
+        quantise_x(0)
+        for i in range(HALVES):
+            support_matmuls(i)
+            if i + 1 < HALVES:
+                quantise_x(i + 1)
+            if i + 2 < HALVES:
+                transpose_x(i + 2)
+            else:
+                product(i + 2 - HALVES)
+            if i == HALVES - 1:
+                transpose_w(0)
+            copy_support(i)
+            if i + 2 < HALVES:
+                copy_x(i + 2)
+            if i == HALVES - 1:
+                copy_w(0)
+            quantise_support(i)
+        quantise_w(0)
+        for r in range(PAIRS):
+            if r + 1 < PAIRS:
+                transpose_w(r + 1)
+            output_matmuls(r)
+            if r + 1 < PAIRS:
+                copy_w(r + 1)
+            if r + 2 < PAIRS:
+                product(r + 2)
+            if r + 1 < PAIRS:
+                quantise_w(r + 1)
+            relu_and_store(r)

@@ -41,14 +41,11 @@ def tile_gcn_pa_kernel(tc, x, adj, S, W1, out):
             in_=W1.rearrange("(u q e) h -> q u e h", u=2, e=2),
         )
         x_view = x.rearrange("b (g u p e) k -> b g p u e k", g=NODE_PASSES, u=2, e=2)
-        x_rows = []
+        x_rows = {}
         for i in range(HALVES):
-            rows = keep.tile([P, PACK, FEATURES], BF16, name="x_rows%d" % i)
-            nc.sync.dma_start(
-                out=rows[:].rearrange("p (u e) k -> p u e k", u=2),
-                in_=x_view[i // NODE_PASSES, i % NODE_PASSES],
-            )
-            x_rows.append(rows)
+            for u in range(2):
+                x_rows[(i, u)] = keep.tile([P, 2, FEATURES], BF16, name="x_rows%d_%d" % (i, u))
+                nc.sync.dma_start(out=x_rows[(i, u)][:], in_=x_view[i // NODE_PASSES, i % NODE_PASSES, :, u])
         adj_view = adj.rearrange("(p t) m -> p t m", t=NODE_TILES)
         s_view = S.rearrange("(p t) m -> p t m", t=NODE_TILES)
         out_view = out.rearrange("b (p t) h -> b p t h", t=NODE_TILES)
@@ -98,9 +95,8 @@ def tile_gcn_pa_kernel(tc, x, adj, S, W1, out):
         sup_q = {}
 
         def transpose_x(i):
-            words = x_rows[i][:].bitcast(F32)
             x_banks[i] = [
-                transpose_words(words[:, 2 * u : 2 * u + 2, :].rearrange("p e w -> p (e w)")) for u in range(2)
+                transpose_words(x_rows[(i, u)][:].bitcast(F32).rearrange("p e w -> p (e w)")) for u in range(2)
             ]
 
         def copy_x(i):
@@ -195,12 +191,15 @@ def tile_gcn_pa_kernel(tc, x, adj, S, W1, out):
 
         def relu_and_store(r):
             for b in range(BATCH):
-                result = keep.tile([P, 2, HIDDEN], F32, name="result%d_%d" % (r, b))
-                nc.scalar.activation(
-                    out=result[:, 0, :], in_=out_banks[(r, b, 0)][:], func=mybir.ActivationFunctionType.Relu
-                )
-                nc.vector.tensor_scalar_max(out=result[:, 1, :], in0=out_banks[(r, b, 1)][:], scalar1=0.0)
-                nc.sync.dma_start(out=out_view[b, :, 2 * r : 2 * r + 2, :], in_=result[:])
+                for t in range(2):
+                    result = keep.tile([P, HIDDEN], F32, name="result%d_%d_%d" % (r, b, t))
+                    if b == BATCH - 1 and t == 1:
+                        nc.vector.tensor_scalar_max(out=result[:], in0=out_banks[(r, b, t)][:], scalar1=0.0)
+                    else:
+                        nc.scalar.activation(
+                            out=result[:], in_=out_banks[(r, b, t)][:], func=mybir.ActivationFunctionType.Relu
+                        )
+                    nc.sync.dma_start(out=out_view[b, :, 2 * r + t, :], in_=result[:])
 
         transpose_x(0)
         copy_x(0)
@@ -213,13 +212,13 @@ def tile_gcn_pa_kernel(tc, x, adj, S, W1, out):
                 quantise_x(i + 1)
             if i + 2 < HALVES:
                 transpose_x(i + 2)
-            else:
-                product(i + 2 - HALVES)
             if i == HALVES - 1:
                 transpose_w(0)
             copy_support(i)
             if i + 2 < HALVES:
                 copy_x(i + 2)
+            else:
+                product(i + 2 - HALVES)
             if i == HALVES - 1:
                 copy_w(0)
             quantise_support(i)

from contextlib import ExitStack

import concourse.mybir as mybir
from concourse.masks import make_identity

BF16 = mybir.dt.bfloat16
F32 = mybir.dt.float32
U32 = mybir.dt.uint32
U8 = mybir.dt.uint8
FP8X4 = mybir.dt.float8_e4m3fn_x4

P = 128
PACK = 4
K_PASS = P * PACK

BATCH = 2
NODES = 1024
FEATURES = 512
HIDDEN = 512
NODE_PASSES = NODES // K_PASS
HALVES = BATCH * NODE_PASSES
NODE_TILES = NODES // P
PAIRS = NODE_TILES // 2
QUARTERS = HIDDEN // P

FLOPS = 2 * BATCH * NODES * FEATURES * HIDDEN + 2 * BATCH * NODES * NODES * HIDDEN


def tile_gcn_pa_kernel(tc, x, adj, S, W1, out):
    nc = tc.nc

    with ExitStack() as ctx:
        ctx.enter_context(tc.manual_schedule())
        keep = ctx.enter_context(tc.tile_pool(name="keep", bufs=1))
        tr_psum = ctx.enter_context(tc.psum_pool(name="tr_psum", bufs=4))
        mm_psum = ctx.enter_context(tc.psum_pool(name="mm_psum", bufs=4))

        w1_rows = keep.tile([P, PACK, HIDDEN], BF16, name="w1_rows")
        nc.sync.dma_start(
            out=w1_rows[:].rearrange("q (u e) h -> q u e h", u=2),
            in_=W1.rearrange("(u q e) h -> q u e h", u=2, e=2),
        )
        x_view = x.rearrange("b (g u p e) k -> b g p u e k", g=NODE_PASSES, u=2, e=2)
        x_rows = {}
        for i in range(HALVES):
            for u in range(2):
                x_rows[(i, u)] = keep.tile([P, 2, FEATURES], BF16, name="x_rows%d_%d" % (i, u))
                nc.sync.dma_start(out=x_rows[(i, u)][:], in_=x_view[i // NODE_PASSES, i % NODE_PASSES, :, u])
        adj_view = adj.rearrange("(p t) m -> p t m", t=NODE_TILES)
        s_view = S.rearrange("(p t) m -> p t m", t=NODE_TILES)
        out_view = out.rearrange("b (p t) h -> b p t h", t=NODE_TILES)
        adj_rows = []
        s_rows = []
        for r in range(PAIRS):
            a = keep.tile([P, 2, NODES], BF16, name="adj_rows%d" % r)
            nc.sync.dma_start(out=a[:], in_=adj_view[:, 2 * r : 2 * r + 2, :])
            adj_rows.append(a)
            s = keep.tile([P, 2, NODES], BF16, name="s_rows%d" % r)
            nc.sync.dma_start(out=s[:], in_=s_view[:, 2 * r : 2 * r + 2, :])
            s_rows.append(s)

        ident = keep.tile([P, P], F32, name="ident")
        make_identity(nc, ident[:])

        w1_grouped = keep.tile([P, HIDDEN, PACK], BF16, name="w1_grouped", align_bytes=64)
        nc.vector.tensor_copy(
            out=w1_grouped[:].rearrange("q (c i) t -> q c t i", i=4),
            in_=w1_rows[:].rearrange("q t (c i) -> q c t i", i=4),
        )
        w1_codes = keep.tile([P, HIDDEN], U32, name="w1_codes", align_bytes=64)
        w1_scales = keep.tile([P, HIDDEN], U8, name="w1_scales", align_bytes=64)
        nc.vector.quantize_mx(
            out=w1_codes[:].bitcast(FP8X4),
            scales=w1_scales[:],
            in_=w1_grouped[:].rearrange("q h t -> q (h t)"),
        )

        def quantise(name, grouped):
            codes = keep.tile([P, K_PASS], U32, name=name + "_codes", align_bytes=64)
            scales = keep.tile([P, K_PASS], U8, name=name + "_scales", align_bytes=64)
            nc.vector.quantize_mx(out=codes[:].bitcast(FP8X4), scales=scales[:], in_=grouped)
            return codes, scales

        def transpose_words(rows):
            bank = tr_psum.tile([P, PACK, P], F32, tag="tr", name="tr_bank")
            for c in range(PACK):
                nc.tensor.transpose(bank[:, c, :], rows[:, c * P : (c + 1) * P], ident[:])
            return bank

        x_banks = {}
        x_grouped = {}
        x_q = {}
        sup_banks = {}
        sup_grouped = {}
        sup_q = {}

        def transpose_x(i):
            x_banks[i] = [
                transpose_words(x_rows[(i, u)][:].bitcast(F32).rearrange("p e w -> p (e w)")) for u in range(2)
            ]

        def copy_x(i):
            x_grouped[i] = keep.tile([P, PACK, P, PACK], BF16, name="x_grouped%d" % i, align_bytes=64)
            for u in range(2):
                nc.scalar.copy(
                    out=x_grouped[i][:, 2 * u : 2 * u + 2, :, :].bitcast(F32),
                    in_=x_banks[i][u][:].rearrange("q (e uk) m -> q e m uk", e=2),
                )

        def quantise_x(i):
            x_q[i] = quantise("x%d" % i, x_grouped[i][:].rearrange("q j m t -> q (j m t)"))

        def support_matmuls(i):
            codes, scales = x_q[i]
            sup_banks[i] = []
            for hq in range(QUARTERS):
                h_cols = slice(hq * P, (hq + 1) * P)
                bank = mm_psum.tile([P, PACK, P], F32, tag="mm", name="sup_bank")
                for j in range(PACK):
                    m_cols = slice(j * P, (j + 1) * P)
                    nc.tensor.matmul_mx(
                        out=bank[:, j, :],
                        lhsT=codes[:, m_cols].bitcast(FP8X4),
                        lhsT_scale=scales[:, m_cols],
                        rhs=w1_codes[:, h_cols].bitcast(FP8X4),
                        rhs_scale=w1_scales[:, h_cols],
                        start=True,
                        stop=True,
                    )
                sup_banks[i].append(bank)

        def copy_support(i):
            sup_grouped[i] = keep.tile([P, HIDDEN, PACK], BF16, name="sup_grouped%d" % i, align_bytes=64)
            first_on_vector = 2 if i < NODE_PASSES else 3
            for hq in range(QUARTERS):
                dst = sup_grouped[i][:, hq * P : (hq + 1) * P, :]
                src = sup_banks[i][hq][:].rearrange("p j h -> p h j")
                if hq >= first_on_vector:
                    nc.vector.tensor_copy(out=dst, in_=src)
                else:
                    nc.scalar.copy(out=dst, in_=src)

        def quantise_support(i):
            sup_q[i] = quantise("sup%d" % i, sup_grouped[i][:].rearrange("p h j -> p (h j)"))

        w_rows = {}
        w_banks = {}
        w_grouped = {}
        w_q = {}
        out_banks = {}

        def product(r):
            w_rows[r] = keep.tile([P, 2, NODES], BF16, name="w_rows%d" % r)
            nc.vector.tensor_tensor(
                out=w_rows[r][:], in0=adj_rows[r][:], in1=s_rows[r][:], op=mybir.AluOpType.mult
            )

        def transpose_w(r):
            words = w_rows[r][:].bitcast(F32)
            w_banks[r] = [transpose_words(words[:, t, :]) for t in range(2)]

        def copy_w(r):
            w_grouped[r] = keep.tile([P, 2, NODE_PASSES, P, PACK], BF16, name="w_grouped%d" % r, align_bytes=64)
            for t in range(2):
                nc.scalar.copy(
                    out=w_grouped[r][:, t, :, :, :].bitcast(F32),
                    in_=w_banks[r][t][:].rearrange("p (g u) n -> p g n u", g=NODE_PASSES),
                )

        def quantise_w(r):
            w_q[r] = quantise("w%d" % r, w_grouped[r][:].rearrange("p t g n v -> p (t g n v)"))

        def output_matmuls(r):
            codes, scales = w_q[r]
            for b in range(BATCH):
                for t in range(2):
                    bank = mm_psum.tile([P, HIDDEN], F32, tag="mm", name="out_bank")
                    for g in range(NODE_PASSES):
                        n_cols = slice((t * NODE_PASSES + g) * P, (t * NODE_PASSES + g + 1) * P)
                        s_codes, s_scales = sup_q[b * NODE_PASSES + g]
                        nc.tensor.matmul_mx(
                            out=bank[:],
                            lhsT=codes[:, n_cols].bitcast(FP8X4),
                            lhsT_scale=scales[:, n_cols],
                            rhs=s_codes[:].bitcast(FP8X4),
                            rhs_scale=s_scales[:],
                            start=(g == 0),
                            stop=(g == NODE_PASSES - 1),
                        )
                    out_banks[(r, b, t)] = bank

        def relu_and_store(r):
            for b in range(BATCH):
                for t in range(2):
                    result = keep.tile([P, HIDDEN], F32, name="result%d_%d_%d" % (r, b, t))
                    if b == BATCH - 1 and t == 1:
                        nc.vector.tensor_scalar_max(out=result[:], in0=out_banks[(r, b, t)][:], scalar1=0.0)
                    else:
                        nc.scalar.activation(
                            out=result[:], in_=out_banks[(r, b, t)][:], func=mybir.ActivationFunctionType.Relu
                        )
                    nc.sync.dma_start(out=out_view[b, :, 2 * r + t, :], in_=result[:])

        transpose_x(0)
        copy_x(0)
        transpose_x(1)
        copy_x(1)
        quantise_x(0)
        for i in range(HALVES):
            support_matmuls(i)
            if i + 1 < HALVES:
                quantise_x(i + 1)
            if i + 2 < HALVES:
                transpose_x(i + 2)
            if i == HALVES - 1:
                transpose_w(0)
            copy_support(i)
            if i + 2 < HALVES:
                copy_x(i + 2)
            else:
                product(i + 2 - HALVES)
            if i == HALVES - 1:
                copy_w(0)
            quantise_support(i)
        quantise_w(0)
        for r in range(PAIRS):
            if r + 1 < PAIRS:
                transpose_w(r + 1)
            output_matmuls(r)
            if r + 1 < PAIRS:
                copy_w(r + 1)
            if r + 2 < PAIRS:
                product(r + 2)
            if r + 1 < PAIRS:
                quantise_w(r + 1)
            relu_and_store(r)
